import numpy as np
import ml_dtypes

BF16 = ml_dtypes.bfloat16


def bf(x):
    return np.asarray(x, np.float32).astype(BF16)


def f32(x):
    return np.asarray(x, np.float32)


def f64(x):
    return np.asarray(x).astype(np.float64)


def striped(idx):
    return np.tile(idx.reshape(-1, 16).T, (8, 1))


V, D, M, N, NC, CD = 2048, 128, 128, 1792, 4, 32
EPS = 1e-12


def setup_inputs():
    return {"table": bf(np.random.standard_normal((D, V))), "w": bf(np.random.standard_normal((D, M)) / np.sqrt(D)), "b": f32(0.2 * np.random.standard_normal((M, 1))), "offs": striped(np.random.permutation(np.tile(np.arange(V), 2))[:N])}


def reference(table, w, b, offs):
    idx = offs[:16].T.reshape(-1)
    z = f64(w).T @ f64(table)[:, idx] + f64(b)
    zc = z.reshape(NC, CD, -1)
    nrm = np.sqrt((zc ** 2).sum(axis=1, keepdims=True))
    return (zc / np.maximum(nrm, EPS)).reshape(M, -1)

@@ -1,0 +1,66 @@
+import concourse.mybir as mybir
+
+BF16, F32, U16 = mybir.dt.bfloat16, mybir.dt.float32, mybir.dt.uint16
+ADD, MULT = mybir.AluOpType.add, mybir.AluOpType.mult
+SQUARE = mybir.ActivationFunctionType.Square
+ABS_RSQRT = mybir.ActivationFunctionType.Abs_reciprocal_sqrt
+
+P = 128
+V = 2048
+N = 1792
+CD = 32
+EPS = 1e-12
+PIECE = 448
+PIECES = N // PIECE
+PIECE_OFFS = PIECE // 16
+
+FLOPS = 2 * P * P * N
+
+
+def tile_conv_kernel(tc, table, w, b, offs, out):
+    nc = tc.nc
+    with (
+        tc.tile_pool(name="held", bufs=1) as held,
+        tc.tile_pool(name="work", bufs=PIECES) as work,
+        tc.psum_pool(name="psum", bufs=PIECES) as psum,
+    ):
+        offsets = held.tile([P, N // 16], U16, name="offsets")
+        nc.sync.dma_start(offsets[:], offs)
+        table_sb = held.tile([P, V], BF16, name="table_sb")
+        nc.scalar.dma_start(table_sb[:], table)
+        w_sb = held.tile([P, P], BF16, name="w_sb")
+        nc.sync.dma_start(w_sb[:], w)
+        b_sb = held.tile([P, 1], F32, name="b_sb")
+        nc.sync.dma_start(b_sb[:], b)
+
+        eps_squared = held.tile([P, 1], F32, name="eps_squared")
+        nc.vector.memset(eps_squared[:], EPS * EPS)
+        cap = held.tile([P, 1], F32, name="cap")
+        nc.scalar.activation(cap[:], eps_squared[:], ABS_RSQRT)
+
+        same_channel = held.tile([P, P], BF16, name="same_channel")
+        nc.gpsimd.memset(same_channel[:], 0.0)
+        for q in range(P // CD):
+            channel = slice(q * CD, (q + 1) * CD)
+            nc.gpsimd.memset(same_channel[channel, channel], 1.0)
+
+        for i in range(PIECES):
+            picked = table_sb[:].indirect(offsets[:, i * PIECE_OFFS : (i + 1) * PIECE_OFFS])
+            wx = psum.tile([P, PIECE], F32, name="wx")
+            nc.tensor.matmul(wx[:], w_sb[:], picked, start=True, stop=True)
+
+            squares = work.tile([P, PIECE], BF16, name="squares")
+            nc.scalar.activation(squares[:], wx[:], SQUARE, bias=b_sb[:, 0:1])
+            nrm_squared = psum.tile([P, PIECE], F32, name="nrm_squared")
+            nc.tensor.matmul(nrm_squared[:], same_channel[:], squares[:], start=True, stop=True)
+
+            rsqrt = work.tile([P, PIECE], F32, name="rsqrt")
+            nc.scalar.activation(rsqrt[:], nrm_squared[:], ABS_RSQRT)
+            inverse = work.tile([P, PIECE], F32, name="inverse")
+            nc.vector.tensor_scalar_min(inverse[:], rsqrt[:], cap[:, 0:1])
+
+            normed = work.tile([P, PIECE], F32, name="normed")
+            nc.vector.scalar_tensor_tensor(
+                normed[:], wx[:], b_sb[:, 0:1], inverse[:], op0=ADD, op1=MULT
+            )
+            nc.sync.dma_start(out[:, i * PIECE : (i + 1) * PIECE], normed[:])

@@ -13,6 +13,7 @@ EPS = 1e-12
 PIECE = 448
 PIECES = N // PIECE
 PIECE_OFFS = PIECE // 16
+WARM_UPS = 6
 
 FLOPS = 2 * P * P * N
 
@@ -43,6 +44,12 @@ def tile_conv_kernel(tc, table, w, b, offs, out):
         for q in range(P // CD):
             channel = slice(q * CD, (q + 1) * CD)
             nc.gpsimd.memset(same_channel[channel, channel], 1.0)
+
+        zeros = held.tile([P, PIECE], BF16, name="zeros")
+        nc.gpsimd.memset(zeros[:], 0.0)
+        unread = psum.tile([P, PIECE], F32, name="unread", tag="wx")
+        for k in range(WARM_UPS):
+            nc.tensor.matmul(unread[:], zeros[:, 0:P], zeros[:], start=True, stop=True)
 
         for i in range(PIECES):
             picked = table_sb[:].indirect(offsets[:, i * PIECE_OFFS : (i + 1) * PIECE_OFFS])

@@ -1,7 +1,7 @@
 import concourse.mybir as mybir
 
 BF16, F32, U16 = mybir.dt.bfloat16, mybir.dt.float32, mybir.dt.uint16
-ADD, MULT = mybir.AluOpType.add, mybir.AluOpType.mult
+MIN, MULT = mybir.AluOpType.min, mybir.AluOpType.mult
 SQUARE = mybir.ActivationFunctionType.Square
 ABS_RSQRT = mybir.ActivationFunctionType.Abs_reciprocal_sqrt
 
@@ -13,7 +13,6 @@ EPS = 1e-12
 PIECE = 448
 PIECES = N // PIECE
 PIECE_OFFS = PIECE // 16
-WARM_UPS = 6
 
 FLOPS = 2 * P * P * N
 
@@ -45,12 +44,6 @@ def tile_conv_kernel(tc, table, w, b, offs, out):
             channel = slice(q * CD, (q + 1) * CD)
             nc.gpsimd.memset(same_channel[channel, channel], 1.0)
 
-        zeros = held.tile([P, PIECE], BF16, name="zeros")
-        nc.gpsimd.memset(zeros[:], 0.0)
-        unread = psum.tile([P, PIECE], F32, name="unread", tag="wx")
-        for k in range(WARM_UPS):
-            nc.tensor.matmul(unread[:], zeros[:, 0:P], zeros[:], start=True, stop=True)
-
         for i in range(PIECES):
             picked = table_sb[:].indirect(offsets[:, i * PIECE_OFFS : (i + 1) * PIECE_OFFS])
             wx = psum.tile([P, PIECE], F32, name="wx")
@@ -58,16 +51,15 @@ def tile_conv_kernel(tc, table, w, b, offs, out):
 
             squares = work.tile([P, PIECE], BF16, name="squares")
             nc.scalar.activation(squares[:], wx[:], SQUARE, bias=b_sb[:, 0:1])
+            z = work.tile([P, PIECE], F32, name="z")
+            nc.vector.tensor_scalar_add(z[:], wx[:], b_sb[:, 0:1])
             nrm_squared = psum.tile([P, PIECE], F32, name="nrm_squared")
             nc.tensor.matmul(nrm_squared[:], same_channel[:], squares[:], start=True, stop=True)
 
             rsqrt = work.tile([P, PIECE], F32, name="rsqrt")
             nc.scalar.activation(rsqrt[:], nrm_squared[:], ABS_RSQRT)
-            inverse = work.tile([P, PIECE], F32, name="inverse")
-            nc.vector.tensor_scalar_min(inverse[:], rsqrt[:], cap[:, 0:1])
-
             normed = work.tile([P, PIECE], F32, name="normed")
             nc.vector.scalar_tensor_tensor(
-                normed[:], wx[:], b_sb[:, 0:1], inverse[:], op0=ADD, op1=MULT
+                normed[:], rsqrt[:], cap[:, 0:1], z[:], op0=MIN, op1=MULT
             )
             nc.sync.dma_start(out[:, i * PIECE : (i + 1) * PIECE], normed[:])

@@ -11,8 +11,8 @@ N = 1792
 CD = 32
 EPS = 1e-12
 PIECE = 448
-PIECES = N // PIECE
-PIECE_OFFS = PIECE // 16
+WIDTHS = (PIECE // 2,) + (PIECE,) * (N // PIECE - 1) + (PIECE // 2,)
+NRM_BUFS = 8 - len(WIDTHS)
 
 FLOPS = 2 * P * P * N
 
@@ -21,8 +21,9 @@ def tile_conv_kernel(tc, table, w, b, offs, out):
     nc = tc.nc
     with (
         tc.tile_pool(name="held", bufs=1) as held,
-        tc.tile_pool(name="work", bufs=PIECES) as work,
-        tc.psum_pool(name="psum", bufs=PIECES) as psum,
+        tc.tile_pool(name="work", bufs=len(WIDTHS)) as work,
+        tc.psum_pool(name="psum_wx", bufs=len(WIDTHS)) as psum_wx,
+        tc.psum_pool(name="psum_nrm", bufs=NRM_BUFS) as psum_nrm,
     ):
         offsets = held.tile([P, N // 16], U16, name="offsets")
         nc.sync.dma_start(offsets[:], offs)
@@ -44,22 +45,24 @@ def tile_conv_kernel(tc, table, w, b, offs, out):
             channel = slice(q * CD, (q + 1) * CD)
             nc.gpsimd.memset(same_channel[channel, channel], 1.0)
 
-        for i in range(PIECES):
-            picked = table_sb[:].indirect(offsets[:, i * PIECE_OFFS : (i + 1) * PIECE_OFFS])
-            wx = psum.tile([P, PIECE], F32, name="wx")
+        first = 0
+        for width in WIDTHS:
+            picked = table_sb[:].indirect(offsets[:, first // 16 : (first + width) // 16])
+            wx = psum_wx.tile([P, width], F32, name="wx")
             nc.tensor.matmul(wx[:], w_sb[:], picked, start=True, stop=True)
 
-            squares = work.tile([P, PIECE], BF16, name="squares")
+            squares = work.tile([P, width], BF16, name="squares")
             nc.scalar.activation(squares[:], wx[:], SQUARE, bias=b_sb[:, 0:1])
-            z = work.tile([P, PIECE], F32, name="z")
+            z = work.tile([P, width], F32, name="z")
             nc.vector.tensor_scalar_add(z[:], wx[:], b_sb[:, 0:1])
-            nrm_squared = psum.tile([P, PIECE], F32, name="nrm_squared")
+            nrm_squared = psum_nrm.tile([P, width], F32, name="nrm_squared")
             nc.tensor.matmul(nrm_squared[:], same_channel[:], squares[:], start=True, stop=True)
 
-            rsqrt = work.tile([P, PIECE], F32, name="rsqrt")
+            rsqrt = work.tile([P, width], F32, name="rsqrt")
             nc.scalar.activation(rsqrt[:], nrm_squared[:], ABS_RSQRT)
-            normed = work.tile([P, PIECE], F32, name="normed")
+            normed = work.tile([P, width], F32, name="normed")
             nc.vector.scalar_tensor_tensor(
                 normed[:], rsqrt[:], cap[:, 0:1], z[:], op0=MIN, op1=MULT
             )
-            nc.sync.dma_start(out[:, i * PIECE : (i + 1) * PIECE], normed[:])
+            nc.sync.dma_start(out[:, first : first + width], normed[:])
+            first += width

@@ -45,24 +45,28 @@ def tile_conv_kernel(tc, table, w, b, offs, out):
             channel = slice(q * CD, (q + 1) * CD)
             nc.gpsimd.memset(same_channel[channel, channel], 1.0)
 
-        first = 0
-        for width in WIDTHS:
+        pieces = range(len(WIDTHS))
+        firsts = [sum(WIDTHS[:i]) for i in pieces]
+
+        squares, z = [], []
+        for i in pieces:
+            first, width = firsts[i], WIDTHS[i]
             picked = table_sb[:].indirect(offsets[:, first // 16 : (first + width) // 16])
             wx = psum_wx.tile([P, width], F32, name="wx")
             nc.tensor.matmul(wx[:], w_sb[:], picked, start=True, stop=True)
+            squares.append(work.tile([P, width], BF16, name="squares"))
+            nc.scalar.activation(squares[i][:], wx[:], SQUARE, bias=b_sb[:, 0:1])
+            z.append(work.tile([P, width], F32, name="z"))
+            nc.vector.tensor_scalar_add(z[i][:], wx[:], b_sb[:, 0:1])
 
-            squares = work.tile([P, width], BF16, name="squares")
-            nc.scalar.activation(squares[:], wx[:], SQUARE, bias=b_sb[:, 0:1])
-            z = work.tile([P, width], F32, name="z")
-            nc.vector.tensor_scalar_add(z[:], wx[:], b_sb[:, 0:1])
+        for i in pieces:
+            first, width = firsts[i], WIDTHS[i]
             nrm_squared = psum_nrm.tile([P, width], F32, name="nrm_squared")
-            nc.tensor.matmul(nrm_squared[:], same_channel[:], squares[:], start=True, stop=True)
-
+            nc.tensor.matmul(nrm_squared[:], same_channel[:], squares[i][:], start=True, stop=True)
             rsqrt = work.tile([P, width], F32, name="rsqrt")
             nc.scalar.activation(rsqrt[:], nrm_squared[:], ABS_RSQRT)
             normed = work.tile([P, width], F32, name="normed")
             nc.vector.scalar_tensor_tensor(
-                normed[:], rsqrt[:], cap[:, 0:1], z[:], op0=MIN, op1=MULT
+                normed[:], rsqrt[:], cap[:, 0:1], z[i][:], op0=MIN, op1=MULT
             )
             nc.sync.dma_start(out[:, first : first + width], normed[:])
-            first += width

@@ -10,9 +10,11 @@ V = 2048
 N = 1792
 CD = 32
 EPS = 1e-12
-PIECE = 448
-WIDTHS = (PIECE // 2,) + (PIECE,) * (N // PIECE - 1) + (PIECE // 2,)
-NRM_BUFS = 8 - len(WIDTHS)
+BANK = 512
+GATHER_WIDTHS = (BANK,) * (N // BANK) + (N % BANK,)
+SHORT = 128
+NORM_WIDTHS = (SHORT,) + (BANK,) * ((N - 2 * SHORT) // BANK) + (SHORT,)
+assert sum(GATHER_WIDTHS) == N and sum(NORM_WIDTHS) == N
 
 FLOPS = 2 * P * P * N
 
@@ -21,9 +23,8 @@ def tile_conv_kernel(tc, table, w, b, offs, out):
     nc = tc.nc
     with (
         tc.tile_pool(name="held", bufs=1) as held,
-        tc.tile_pool(name="work", bufs=len(WIDTHS)) as work,
-        tc.psum_pool(name="psum_wx", bufs=len(WIDTHS)) as psum_wx,
-        tc.psum_pool(name="psum_nrm", bufs=NRM_BUFS) as psum_nrm,
+        tc.psum_pool(name="psum_wx", bufs=len(GATHER_WIDTHS)) as psum_wx,
+        tc.psum_pool(name="psum_nrm", bufs=8 - len(GATHER_WIDTHS)) as psum_nrm,
     ):
         offsets = held.tile([P, N // 16], U16, name="offsets")
         nc.sync.dma_start(offsets[:], offs)
@@ -45,28 +46,29 @@ def tile_conv_kernel(tc, table, w, b, offs, out):
             channel = slice(q * CD, (q + 1) * CD)
             nc.gpsimd.memset(same_channel[channel, channel], 1.0)
 
-        pieces = range(len(WIDTHS))
-        firsts = [sum(WIDTHS[:i]) for i in pieces]
+        squares = held.tile([P, N], BF16, name="squares")
+        z = held.tile([P, N], F32, name="z")
+        rsqrt = held.tile([P, N], F32, name="rsqrt")
+        normed = held.tile([P, N], F32, name="normed")
 
-        squares, z = [], []
-        for i in pieces:
-            first, width = firsts[i], WIDTHS[i]
+        first = 0
+        for width in GATHER_WIDTHS:
+            piece = slice(first, first + width)
             picked = table_sb[:].indirect(offsets[:, first // 16 : (first + width) // 16])
             wx = psum_wx.tile([P, width], F32, name="wx")
             nc.tensor.matmul(wx[:], w_sb[:], picked, start=True, stop=True)
-            squares.append(work.tile([P, width], BF16, name="squares"))
-            nc.scalar.activation(squares[i][:], wx[:], SQUARE, bias=b_sb[:, 0:1])
-            z.append(work.tile([P, width], F32, name="z"))
-            nc.vector.tensor_scalar_add(z[i][:], wx[:], b_sb[:, 0:1])
+            nc.scalar.activation(squares[:, piece], wx[:], SQUARE, bias=b_sb[:, 0:1])
+            nc.vector.tensor_scalar_add(z[:, piece], wx[:], b_sb[:, 0:1])
+            first += width
 
-        for i in pieces:
-            first, width = firsts[i], WIDTHS[i]
+        first = 0
+        for width in NORM_WIDTHS:
+            piece = slice(first, first + width)
             nrm_squared = psum_nrm.tile([P, width], F32, name="nrm_squared")
-            nc.tensor.matmul(nrm_squared[:], same_channel[:], squares[i][:], start=True, stop=True)
-            rsqrt = work.tile([P, width], F32, name="rsqrt")
-            nc.scalar.activation(rsqrt[:], nrm_squared[:], ABS_RSQRT)
-            normed = work.tile([P, width], F32, name="normed")
+            nc.tensor.matmul(nrm_squared[:], same_channel[:], squares[:, piece], start=True, stop=True)
+            nc.scalar.activation(rsqrt[:, piece], nrm_squared[:], ABS_RSQRT)
             nc.vector.scalar_tensor_tensor(
-                normed[:], rsqrt[:], cap[:, 0:1], z[i][:], op0=MIN, op1=MULT
+                normed[:, piece], rsqrt[:, piece], cap[:, 0:1], z[:, piece], op0=MIN, op1=MULT
             )
-            nc.sync.dma_start(out[:, first : first + width], normed[:])
+            nc.sync.dma_start(out[:, piece], normed[:, piece])
+            first += width

@@ -10,10 +10,8 @@ V = 2048
 N = 1792
 CD = 32
 EPS = 1e-12
-BANK = 512
-GATHER_WIDTHS = (BANK,) * (N // BANK) + (N % BANK,)
-SHORT = 128
-NORM_WIDTHS = (SHORT,) + (BANK,) * ((N - 2 * SHORT) // BANK) + (SHORT,)
+GATHER_WIDTHS = (224, 448, 448, 448, 224)
+NORM_WIDTHS = (256,) * 7
 assert sum(GATHER_WIDTHS) == N and sum(NORM_WIDTHS) == N
 
 FLOPS = 2 * P * P * N

@@ -10,7 +10,7 @@ V = 2048
 N = 1792
 CD = 32
 EPS = 1e-12
-GATHER_WIDTHS = (224, 448, 448, 448, 224)
+GATHER_WIDTHS = (448,) * 4
 NORM_WIDTHS = (256,) * 7
 assert sum(GATHER_WIDTHS) == N and sum(NORM_WIDTHS) == N
 

@@ -11,7 +11,7 @@ N = 1792
 CD = 32
 EPS = 1e-12
 GATHER_WIDTHS = (448,) * 4
-NORM_WIDTHS = (256,) * 7
+NORM_WIDTHS = GATHER_WIDTHS
 assert sum(GATHER_WIDTHS) == N and sum(NORM_WIDTHS) == N
 
 FLOPS = 2 * P * P * N

@@ -39,10 +39,10 @@ def tile_conv_kernel(tc, table, w, b, offs, out):
         nc.scalar.activation(cap[:], eps_squared[:], ABS_RSQRT)
 
         same_channel = held.tile([P, P], BF16, name="same_channel")
-        nc.gpsimd.memset(same_channel[:], 0.0)
+        nc.vector.memset(same_channel[:], 0.0)
         for q in range(P // CD):
             channel = slice(q * CD, (q + 1) * CD)
-            nc.gpsimd.memset(same_channel[channel, channel], 1.0)
+            nc.vector.memset(same_channel[channel, channel], 1.0)
 
         squares = held.tile([P, N], BF16, name="squares")
         z = held.tile([P, N], F32, name="z")

@@ -24,10 +24,10 @@ def tile_conv_kernel(tc, table, w, b, offs, out):
         tc.psum_pool(name="psum_wx", bufs=len(GATHER_WIDTHS)) as psum_wx,
         tc.psum_pool(name="psum_nrm", bufs=8 - len(GATHER_WIDTHS)) as psum_nrm,
     ):
+        table_sb = held.tile([P, V], BF16, name="table_sb")
+        nc.sync.dma_start(table_sb[:], table)
         offsets = held.tile([P, N // 16], U16, name="offsets")
         nc.sync.dma_start(offsets[:], offs)
-        table_sb = held.tile([P, V], BF16, name="table_sb")
-        nc.scalar.dma_start(table_sb[:], table)
         w_sb = held.tile([P, P], BF16, name="w_sb")
         nc.sync.dma_start(w_sb[:], w)
         b_sb = held.tile([P, 1], F32, name="b_sb")

import concourse.mybir as mybir

BF16, F32, U16 = mybir.dt.bfloat16, mybir.dt.float32, mybir.dt.uint16
MIN, MULT = mybir.AluOpType.min, mybir.AluOpType.mult
SQUARE = mybir.ActivationFunctionType.Square
ABS_RSQRT = mybir.ActivationFunctionType.Abs_reciprocal_sqrt

P = 128
V = 2048
N = 1792
CD = 32
EPS = 1e-12
GATHER_WIDTHS = (448,) * 4
NORM_WIDTHS = GATHER_WIDTHS
assert sum(GATHER_WIDTHS) == N and sum(NORM_WIDTHS) == N

FLOPS = 2 * P * P * N


def tile_conv_kernel(tc, table, w, b, offs, out):
    nc = tc.nc
    with (
        tc.tile_pool(name="held", bufs=1) as held,
        tc.psum_pool(name="psum_wx", bufs=len(GATHER_WIDTHS)) as psum_wx,
        tc.psum_pool(name="psum_nrm", bufs=8 - len(GATHER_WIDTHS)) as psum_nrm,
    ):
        table_sb = held.tile([P, V], BF16, name="table_sb")
        nc.sync.dma_start(table_sb[:], table)
        offsets = held.tile([P, N // 16], U16, name="offsets")
        nc.sync.dma_start(offsets[:], offs)
        w_sb = held.tile([P, P], BF16, name="w_sb")
        nc.sync.dma_start(w_sb[:], w)
        b_sb = held.tile([P, 1], F32, name="b_sb")
        nc.sync.dma_start(b_sb[:], b)

        eps_squared = held.tile([P, 1], F32, name="eps_squared")
        nc.vector.memset(eps_squared[:], EPS * EPS)
        cap = held.tile([P, 1], F32, name="cap")
        nc.scalar.activation(cap[:], eps_squared[:], ABS_RSQRT)

        same_channel = held.tile([P, P], BF16, name="same_channel")
        nc.vector.memset(same_channel[:], 0.0)
        for q in range(P // CD):
            channel = slice(q * CD, (q + 1) * CD)
            nc.vector.memset(same_channel[channel, channel], 1.0)

        squares = held.tile([P, N], BF16, name="squares")
        z = held.tile([P, N], F32, name="z")
        rsqrt = held.tile([P, N], F32, name="rsqrt")
        normed = held.tile([P, N], F32, name="normed")

        first = 0
        for width in GATHER_WIDTHS:
            piece = slice(first, first + width)
            picked = table_sb[:].indirect(offsets[:, first // 16 : (first + width) // 16])
            wx = psum_wx.tile([P, width], F32, name="wx")
            nc.tensor.matmul(wx[:], w_sb[:], picked, start=True, stop=True)
            nc.scalar.activation(squares[:, piece], wx[:], SQUARE, bias=b_sb[:, 0:1])
            nc.vector.tensor_scalar_add(z[:, piece], wx[:], b_sb[:, 0:1])
            first += width

        first = 0
        for width in NORM_WIDTHS:
            piece = slice(first, first + width)
            nrm_squared = psum_nrm.tile([P, width], F32, name="nrm_squared")
            nc.tensor.matmul(nrm_squared[:], same_channel[:], squares[:, piece], start=True, stop=True)
            nc.scalar.activation(rsqrt[:, piece], nrm_squared[:], ABS_RSQRT)
            nc.vector.scalar_tensor_tensor(
                normed[:, piece], rsqrt[:, piece], cap[:, 0:1], z[:, piece], op0=MIN, op1=MULT
            )
            nc.sync.dma_start(out[:, piece], normed[:, piece])
            first += width
